import numpy as np
import ml_dtypes


def mxq(x, axis, fmt="e4m3"):
    dtype, down = {"e4m3": (ml_dtypes.float8_e4m3fn, 7), "e5m2": (ml_dtypes.float8_e5m2, 14)}[fmt]
    v = np.moveaxis(np.asarray(x, np.float32).astype(ml_dtypes.bfloat16).astype(np.float64), axis, -1)
    blocks = v.reshape(v.shape[:-1] + (-1, 32))
    amax = np.abs(blocks).max(-1, keepdims=True)
    byte = np.maximum(np.where(amax > 0, np.frexp(amax)[1] - 1 + 127, 0) - down, 1)
    scale = np.exp2(byte - 127.0)
    codes = (blocks / scale).astype(np.float32).astype(dtype).astype(np.float64)
    return np.moveaxis((codes * scale).reshape(v.shape), -1, axis)


WIDE = False


def mx_kscale(k):
    if not WIDE:
        return np.ones(k)
    levels = np.array([10, -10, 5, -5, 0])
    a = np.random.permutation(np.resize(levels, k // 512 * 4)).reshape(k // 512, 4)
    idx = np.arange(k)
    return np.exp2(a[idx // 512, idx % 128 // 32])


BF16 = ml_dtypes.bfloat16


def bf(x):
    return np.asarray(x, np.float32).astype(BF16)


def f64(x):
    return np.asarray(x).astype(np.float64)


E2M1 = np.array([0.0, 0.5, 1.0, 1.5, 2.0, 3.0, 4.0, 6.0, -0.0, -0.5, -1.0, -1.5, -2.0, -3.0, -4.0, -6.0])


def pack_weight(w, fmt):
    k, n = w.shape
    w = f64(bf(w)).reshape(k // 32, 32, n)
    amax = np.abs(w).max(1)
    if fmt == "e4m3":
        byte = np.frexp(amax)[1] - 1 + 127 - 7
    else:
        mant, ex = np.frexp(amax / 6.0)
        byte = np.where(mant > 0.5, ex, ex - 1) + 127
    byte = np.clip(np.where(amax > 0, byte, 1), 1, 254)
    scaled = (w * np.exp2(127.0 - byte)[:, None, :]).reshape(k, n).astype(np.float32)
    by_word = np.ascontiguousarray(scaled.reshape(k // 512, 128, 4, n).transpose(0, 1, 3, 2))
    if fmt == "e4m3":
        words = by_word.astype(ml_dtypes.float8_e4m3fn).view(np.uint8)
    else:
        c = by_word.astype(ml_dtypes.float4_e2m1fn).view(np.uint8) & 0xF
        words = c[..., 0::2] | (c[..., 1::2] << 4)
    return np.ascontiguousarray(words), np.ascontiguousarray(byte.astype(np.uint8).reshape(k // 512, 16, n))


def unpack_weight(words, scales, fmt):
    g, p, n, _ = words.shape
    if fmt == "e4m3":
        vals = np.ascontiguousarray(words).view(ml_dtypes.float8_e4m3fn).astype(np.float64)
    else:
        nib = np.empty((g, p, n, 4), np.uint8)
        nib[..., 0::2] = words & 0xF
        nib[..., 1::2] = words >> 4
        vals = E2M1[nib]
    vals = vals * np.repeat(np.exp2(scales.astype(np.float64) - 127.0), 8, axis=1)[..., None]
    return vals.transpose(0, 1, 3, 2).reshape(g * 512, n)


N, D, O, H, W = 2, 8192, 256, 16, 16
K = D + D
P = H * W


def exp_softmax_pool(y):
    a = np.exp(y)
    e = np.exp(a - a.max(-1, keepdims=True))
    sm = e / e.sum(-1, keepdims=True)
    return (sm * y).sum(-1)


def setup_inputs():
    s = mx_kscale(K)
    x1 = bf(np.random.standard_normal((N, D, H, W)) * 0.5 * s[:D][None, :, None, None])
    x2 = bf(np.random.standard_normal((N, D, H, W)) * 0.5 * s[D:][None, :, None, None])
    c1_w_words, c1_w_scales = pack_weight((np.random.standard_normal((O, K)) / np.sqrt(K) / s).T, "e4m3")
    c1_b = bf(np.random.standard_normal(O) * 0.3)
    c2_w_words, c2_w_scales = pack_weight((np.random.standard_normal((O, K)) / np.sqrt(K) / s).T, "e4m3")
    c2_b = bf(np.random.standard_normal(O) * 0.3)
    return {"x1": x1,
            "x2": x2,
            "c1_w_words": c1_w_words, "c1_w_scales": c1_w_scales, "c1_b": c1_b,
            "c2_w_words": c2_w_words, "c2_w_scales": c2_w_scales, "c2_b": c2_b}


def reference(x1, x2, c1_w_words, c1_w_scales, c1_b, c2_w_words, c2_w_scales, c2_b):
    xc = np.concatenate([f64(x1), f64(x2)], axis=1).reshape(N, K, P)
    xq = mxq(xc, 1, "e4m3")
    x1x = (unpack_weight(c1_w_words, c1_w_scales, "e4m3").T @ xq) + f64(c1_b)[None, :, None]
    x2x = (unpack_weight(c2_w_words, c2_w_scales, "e4m3").T @ xq) + f64(c2_b)[None, :, None]
    return exp_softmax_pool(x1x), exp_softmax_pool(x2x)

@@ -1,0 +1,227 @@
+import concourse.mybir as mybir
+from concourse.masks import make_identity
+
+F32 = mybir.dt.float32
+BF16 = mybir.dt.bfloat16
+I32 = mybir.dt.int32
+U32 = mybir.dt.uint32
+U8 = mybir.dt.uint8
+FP8X4 = mybir.dt.float8_e4m3fn_x4
+EXP = mybir.ActivationFunctionType.Exp
+ALU = mybir.AluOpType
+
+P = 128
+PACK = 4
+K_GROUP = P * PACK
+
+IMAGES = 2
+STREAM_CHANNELS = 8192
+POSITIONS = 256
+COLUMNS = IMAGES * POSITIONS
+OUT_CHANNELS = 256
+WEIGHTS = 2
+HALVES = OUT_CHANNELS // P
+BANKS = WEIGHTS * HALVES
+
+STREAM_GROUPS = STREAM_CHANNELS // K_GROUP
+GROUPS = 2 * STREAM_GROUPS
+PAIR = 2
+PAIRS = GROUPS // PAIR
+SCALE_ROWS = 16
+QUADRANTS = 4
+
+RUN = 4
+
+FLOPS = 2 * IMAGES * POSITIONS * (2 * STREAM_CHANNELS) * (WEIGHTS * OUT_CHANNELS)
+
+
+def tile_fr_pa_k_kernel(
+    tc, x1, x2, c1_w_words, c1_w_scales, c1_b, c2_w_words, c2_w_scales, c2_b, out_0, out_1
+):
+    nc = tc.nc
+
+    x_views = [
+        x.rearrange("n (g p t) h w -> g p n (t h w)", p=P, t=PACK) for x in (x1, x2)
+    ]
+    word_views = [w.rearrange("g p n t -> p g (n t)") for w in (c1_w_words, c2_w_words)]
+    scale_views = [s.rearrange("g q n -> q g n") for s in (c1_w_scales, c2_w_scales)]
+    bias_views = [b.rearrange("(h p) -> h p", p=P) for b in (c1_b, c2_b)]
+    out_views = [o.rearrange("n (h p) -> (n h) p", p=P) for o in (out_0, out_1)]
+
+    with tc.tile_pool(name="const", bufs=1) as const, tc.tile_pool(
+        name="weights", bufs=PAIRS
+    ) as weights, tc.tile_pool(name="raw", bufs=6) as raw_pool, tc.tile_pool(
+        name="grouped", bufs=4
+    ) as grouped_pool, tc.tile_pool(name="quantised", bufs=16) as quantised, tc.tile_pool(
+        name="pooling", bufs=BANKS
+    ) as pooling, tc.psum_pool(name="acc", bufs=1) as acc_pool, tc.psum_pool(
+        name="flip", bufs=1
+    ) as flip_pool, tc.manual_schedule():
+        bias_rows = const.tile([P, P], BF16)
+        nc.vector.memset(bias_rows[:], 0.0)
+        for c in range(WEIGHTS):
+            nc.scalar.dma_start(out=bias_rows[HALVES * c : HALVES * (c + 1), :], in_=bias_views[c])
+
+        table_warm = const.tile([P, 1], F32)
+        nc.vector.memset(table_warm[:], 0.0)
+        nc.scalar.activation(out=table_warm[:], in_=table_warm[:], func=EXP)
+
+        identity = const.tile([P, P], F32)
+        make_identity(nc, identity[:])
+
+        w_planes = []
+        for c in range(WEIGHTS):
+            plane = const.tile([P, GROUPS, OUT_CHANNELS], U8, name="w_plane%d" % c, align_bytes=64)
+            nc.vector.memset(plane[:].rearrange("p g n -> p (g n)").bitcast(I32), 0)
+            w_planes.append(plane)
+        for c in range(WEIGHTS):
+            for quadrant in range(QUADRANTS):
+                nc.gpsimd.dma_start(
+                    out=w_planes[c][32 * quadrant : 32 * quadrant + 4].bitcast(F32),
+                    in_=scale_views[c][4 * quadrant : 4 * quadrant + 4].bitcast(F32),
+                )
+
+        pooled = const.tile([P, P], F32)
+        nc.vector.memset(pooled[:], 0.0)
+
+        bias_rows_f32 = const.tile([P, P], F32)
+        nc.vector.tensor_copy(out=bias_rows_f32[:], in_=bias_rows[:])
+        bias_flipped = flip_pool.tile([P, P], F32)
+        nc.tensor.transpose(bias_flipped[:], bias_rows_f32[:], identity[:])
+        bias = const.tile([P, BANKS], F32)
+        nc.vector.tensor_copy(out=bias[:], in_=bias_flipped[:, 0:BANKS])
+
+        acc = [
+            acc_pool.tile([P, COLUMNS], F32, name="acc%d" % bank) for bank in range(BANKS)
+        ]
+
+        raw_tiles = {}
+        grouped_tiles = {}
+        x_words = {}
+        x_planes = {}
+        w_words = {}
+
+        def load_x(g):
+            raw = raw_pool.tile([P, IMAGES, PACK * POSITIONS], BF16, name="raw")
+            nc.sync.dma_start(out=raw[:], in_=x_views[g // STREAM_GROUPS][g % STREAM_GROUPS])
+            raw_tiles[g] = raw
+
+        def load_weights(pair):
+            words = weights.tile([P, WEIGHTS, PAIR, OUT_CHANNELS], U32, name="words", align_bytes=64)
+            for c in range(WEIGHTS):
+                nc.sync.dma_start(
+                    out=words[:, c].bitcast(I32),
+                    in_=word_views[c][:, PAIR * pair : PAIR * (pair + 1), :].bitcast(I32),
+                )
+            w_words[pair] = words
+
+        def regroup(g, copy):
+            grouped = grouped_pool.tile([P, IMAGES, POSITIONS, PACK], BF16, name="grouped", align_bytes=64)
+            for n in range(IMAGES):
+                copy(
+                    out=grouped[:, n].rearrange("p (c i) t -> p c t i", i=RUN),
+                    in_=raw_tiles[g][:, n].rearrange("p (t c i) -> p c t i", t=PACK, i=RUN),
+                )
+            grouped_tiles[g] = grouped
+
+        def quantise(g):
+            words = quantised.tile([P, COLUMNS], U32, name="x_words", align_bytes=64)
+            plane = quantised.tile([P, COLUMNS], U8, name="x_plane", align_bytes=64)
+            nc.vector.quantize_mx(
+                out=words[:].bitcast(FP8X4),
+                scales=plane[:],
+                in_=grouped_tiles[g][:].rearrange("p n w t -> p (n w t)"),
+            )
+            x_words[g] = words
+            x_planes[g] = plane
+
+        def multiply(pair):
+            for c in range(WEIGHTS):
+                for h in range(HALVES):
+                    for i in range(PAIR):
+                        g = PAIR * pair + i
+                        nc.tensor.matmul_mx(
+                            out=acc[HALVES * c + h][:],
+                            lhsT=w_words[pair][:, c, i, P * h : P * (h + 1)].bitcast(FP8X4),
+                            lhsT_scale=w_planes[c][:, g, P * h : P * (h + 1)],
+                            rhs=x_words[g][:].bitcast(FP8X4),
+                            rhs_scale=x_planes[g][:],
+                            start=(g == 0),
+                            stop=(g == GROUPS - 1),
+                        )
+
+        for g in range(PAIR):
+            load_x(g)
+        for pair in range(PAIRS):
+            if pair + 1 < PAIRS:
+                for i in range(PAIR):
+                    load_x(PAIR * (pair + 1) + i)
+            load_weights(pair)
+            regroup(PAIR * pair, nc.scalar.copy)
+            regroup(PAIR * pair + 1, nc.vector.tensor_copy)
+            quantise(PAIR * pair)
+            quantise(PAIR * pair + 1)
+            multiply(pair)
+
+        sum_e = const.tile([P, IMAGES * BANKS], F32)
+        sum_ey = const.tile([P, IMAGES * BANKS], F32)
+        a_tiles = {}
+        neg_max_tiles = {}
+
+        def first_exponential(bank):
+            a = pooling.tile([P, IMAGES, POSITIONS], F32, name="a")
+            nc.scalar.activation(
+                out=a[:].rearrange("p n w -> p (n w)"),
+                in_=acc[bank][:],
+                func=EXP,
+                bias=bias[:, bank : bank + 1],
+            )
+            neg_max = pooling.tile([P, IMAGES], F32, name="neg_max")
+            nc.vector.tensor_reduce(
+                out=neg_max[:], in_=a[:], axis=mybir.AxisListType.X, op=ALU.max, negate=True
+            )
+            a_tiles[bank] = a
+            neg_max_tiles[bank] = neg_max
+
+        def second_exponential(bank):
+            e = pooling.tile([P, IMAGES, POSITIONS], F32, name="e")
+            ey = pooling.tile([P, IMAGES, POSITIONS], F32, name="ey")
+            c, h = divmod(bank, HALVES)
+            for n in range(IMAGES):
+                column = (c * IMAGES + n) * HALVES + h
+                nc.scalar.activation(
+                    out=e[:, n],
+                    in_=a_tiles[bank][:, n],
+                    func=EXP,
+                    bias=neg_max_tiles[bank][:, n : n + 1],
+                    accum_out=sum_e[:, column : column + 1],
+                )
+            for n in range(IMAGES):
+                column = (c * IMAGES + n) * HALVES + h
+                nc.vector.scalar_tensor_tensor(
+                    out=ey[:, n],
+                    in0=acc[bank][:, POSITIONS * n : POSITIONS * (n + 1)],
+                    scalar=bias[:, bank : bank + 1],
+                    in1=e[:, n],
+                    op0=ALU.add,
+                    op1=ALU.mult,
+                    accum_out=sum_ey[:, column : column + 1],
+                )
+
+        for bank in range(BANKS + 1):
+            if bank < BANKS:
+                first_exponential(bank)
+            if bank >= 1:
+                second_exponential(bank - 1)
+
+        one_over_sum_e = const.tile([P, IMAGES * BANKS], F32)
+        nc.vector.reciprocal(out=one_over_sum_e[:], in_=sum_e[:])
+        nc.vector.tensor_mul(out=pooled[:, 0 : IMAGES * BANKS], in0=sum_ey[:], in1=one_over_sum_e[:])
+
+        pooled_flipped = flip_pool.tile([P, P], F32)
+        nc.tensor.transpose(pooled_flipped[:], pooled[:], identity[:])
+        out_rows = const.tile([P, P], F32)
+        nc.vector.tensor_copy(out=out_rows[:], in_=pooled_flipped[:])
+        rows = IMAGES * HALVES
+        for c in range(WEIGHTS):
+            nc.sync.dma_start(out=out_views[c], in_=out_rows[rows * c : rows * (c + 1), :])

@@ -29,6 +29,9 @@ PAIR = 2
 PAIRS = GROUPS // PAIR
 SCALE_ROWS = 16
 QUADRANTS = 4
+SETS = 4
+SET_GROUPS = GROUPS // SETS
+SCALE_SHIFT = 4
 
 RUN = 4
 
@@ -69,17 +72,24 @@ def tile_fr_pa_k_kernel(
         identity = const.tile([P, P], F32)
         make_identity(nc, identity[:])
 
-        w_planes = []
-        for c in range(WEIGHTS):
-            plane = const.tile([P, GROUPS, OUT_CHANNELS], U8, name="w_plane%d" % c, align_bytes=64)
-            nc.vector.memset(plane[:].rearrange("p g n -> p (g n)").bitcast(I32), 0)
-            w_planes.append(plane)
-        for c in range(WEIGHTS):
-            for quadrant in range(QUADRANTS):
-                nc.gpsimd.dma_start(
-                    out=w_planes[c][32 * quadrant : 32 * quadrant + 4].bitcast(F32),
-                    in_=scale_views[c][4 * quadrant : 4 * quadrant + 4].bitcast(F32),
+        w_planes = {}
+        for s in range(SETS):
+            for c in range(WEIGHTS):
+                plane = const.tile(
+                    [P, SET_GROUPS, OUT_CHANNELS], U8, name="w_plane%d_%d" % (c, s), align_bytes=64
                 )
+                nc.vector.memset(plane[:].rearrange("p g n -> p (g n)").bitcast(I32), 0)
+                w_planes[c, s] = plane
+        for s in range(SETS):
+            for c in range(WEIGHTS):
+                for quadrant in range(QUADRANTS):
+                    first = 32 * quadrant + SCALE_SHIFT * s
+                    nc.gpsimd.dma_start(
+                        out=w_planes[c, s][first : first + 4].bitcast(F32),
+                        in_=scale_views[c][
+                            4 * quadrant : 4 * quadrant + 4, SET_GROUPS * s : SET_GROUPS * (s + 1)
+                        ].bitcast(F32),
+                    )
 
         pooled = const.tile([P, P], F32)
         nc.vector.memset(pooled[:], 0.0)
@@ -143,7 +153,9 @@ def tile_fr_pa_k_kernel(
                         nc.tensor.matmul_mx(
                             out=acc[HALVES * c + h][:],
                             lhsT=w_words[pair][:, c, i, P * h : P * (h + 1)].bitcast(FP8X4),
-                            lhsT_scale=w_planes[c][:, g, P * h : P * (h + 1)],
+                            lhsT_scale=w_planes[c, g // SET_GROUPS][
+                                SCALE_SHIFT * (g // SET_GROUPS) : P, g % SET_GROUPS, P * h : P * (h + 1)
+                            ],
                             rhs=x_words[g][:].bitcast(FP8X4),
                             rhs_scale=x_planes[g][:],
                             start=(g == 0),

@@ -28,7 +28,7 @@ GROUPS = 2 * STREAM_GROUPS
 PAIR = 2
 PAIRS = GROUPS // PAIR
 SCALE_ROWS = 16
-QUADRANTS = 4
+QUADRANT_ROWS = 4
 SETS = 4
 SET_GROUPS = GROUPS // SETS
 SCALE_SHIFT = 4
@@ -82,12 +82,11 @@ def tile_fr_pa_k_kernel(
                 w_planes[c, s] = plane
         for s in range(SETS):
             for c in range(WEIGHTS):
-                for quadrant in range(QUADRANTS):
-                    first = 32 * quadrant + SCALE_SHIFT * s
+                for row in range(QUADRANT_ROWS):
                     nc.gpsimd.dma_start(
-                        out=w_planes[c, s][first : first + 4].bitcast(F32),
+                        out=w_planes[c, s][SCALE_SHIFT * s + row : P : 32].bitcast(F32),
                         in_=scale_views[c][
-                            4 * quadrant : 4 * quadrant + 4, SET_GROUPS * s : SET_GROUPS * (s + 1)
+                            row:SCALE_ROWS:QUADRANT_ROWS, SET_GROUPS * s : SET_GROUPS * (s + 1)
                         ].bitcast(F32),
                     )
 

@@ -27,6 +27,7 @@ STREAM_GROUPS = STREAM_CHANNELS // K_GROUP
 GROUPS = 2 * STREAM_GROUPS
 PAIR = 2
 PAIRS = GROUPS // PAIR
+TAIL = 2
 SCALE_ROWS = 16
 QUADRANT_ROWS = 4
 SETS = 4
@@ -115,14 +116,15 @@ def tile_fr_pa_k_kernel(
             nc.sync.dma_start(out=raw[:], in_=x_views[g // STREAM_GROUPS][g % STREAM_GROUPS])
             raw_tiles[g] = raw
 
-        def load_weights(pair):
-            words = weights.tile([P, WEIGHTS, PAIR, OUT_CHANNELS], U32, name="words", align_bytes=64)
-            for c in range(WEIGHTS):
-                nc.sync.dma_start(
-                    out=words[:, c].bitcast(I32),
-                    in_=word_views[c][:, PAIR * pair : PAIR * (pair + 1), :].bitcast(I32),
+        def load_weights(pair, c):
+            if pair not in w_words:
+                w_words[pair] = weights.tile(
+                    [P, WEIGHTS, PAIR, OUT_CHANNELS], U32, name="words", align_bytes=64
                 )
-            w_words[pair] = words
+            nc.sync.dma_start(
+                out=w_words[pair][:, c].bitcast(I32),
+                in_=word_views[c][:, PAIR * pair : PAIR * (pair + 1), :].bitcast(I32),
+            )
 
         def regroup(g, copy):
             grouped = grouped_pool.tile([P, IMAGES, POSITIONS, PACK], BF16, name="grouped", align_bytes=64)
@@ -144,35 +146,42 @@ def tile_fr_pa_k_kernel(
             x_words[g] = words
             x_planes[g] = plane
 
-        def multiply(pair):
-            for c in range(WEIGHTS):
-                for h in range(HALVES):
-                    for i in range(PAIR):
-                        g = PAIR * pair + i
-                        nc.tensor.matmul_mx(
-                            out=acc[HALVES * c + h][:],
-                            lhsT=w_words[pair][:, c, i, P * h : P * (h + 1)].bitcast(FP8X4),
-                            lhsT_scale=w_planes[c, g // SET_GROUPS][
-                                SCALE_SHIFT * (g // SET_GROUPS) : P, g % SET_GROUPS, P * h : P * (h + 1)
-                            ],
-                            rhs=x_words[g][:].bitcast(FP8X4),
-                            rhs_scale=x_planes[g][:],
-                            start=(g == 0),
-                            stop=(g == GROUPS - 1),
-                        )
+        def multiply(g, c, h):
+            pair, i = divmod(g, PAIR)
+            nc.tensor.matmul_mx(
+                out=acc[HALVES * c + h][:],
+                lhsT=w_words[pair][:, c, i, P * h : P * (h + 1)].bitcast(FP8X4),
+                lhsT_scale=w_planes[c, g // SET_GROUPS][
+                    SCALE_SHIFT * (g // SET_GROUPS) : P, g % SET_GROUPS, P * h : P * (h + 1)
+                ],
+                rhs=x_words[g][:].bitcast(FP8X4),
+                rhs_scale=x_planes[g][:],
+                start=(g == 0),
+                stop=(g == GROUPS - 1),
+            )
 
+        order = [(pair, c) for pair in range(PAIRS - TAIL) for c in range(WEIGHTS)] + [
+            (pair, c) for c in range(WEIGHTS) for pair in range(PAIRS - TAIL, PAIRS)
+        ]
         for g in range(PAIR):
             load_x(g)
-        for pair in range(PAIRS):
-            if pair + 1 < PAIRS:
+        for position, (pair, c) in enumerate(order):
+            if position % WEIGHTS == 0 and position < WEIGHTS * (PAIRS - 1):
                 for i in range(PAIR):
-                    load_x(PAIR * (pair + 1) + i)
-            load_weights(pair)
-            regroup(PAIR * pair, nc.scalar.copy)
-            regroup(PAIR * pair + 1, nc.vector.tensor_copy)
-            quantise(PAIR * pair)
-            quantise(PAIR * pair + 1)
-            multiply(pair)
+                    load_x(PAIR * (position // WEIGHTS + 1) + i)
+            load_weights(pair, c)
+            if c == 0:
+                regroup(PAIR * pair, nc.scalar.copy)
+                regroup(PAIR * pair + 1, nc.vector.tensor_copy)
+                quantise(PAIR * pair)
+                quantise(PAIR * pair + 1)
+            if pair < PAIRS - TAIL or c == 0:
+                for h in range(HALVES):
+                    for i in range(PAIR):
+                        multiply(PAIR * pair + i, c, h)
+        for h in range(HALVES):
+            for g in range(PAIR * (PAIRS - TAIL), GROUPS):
+                multiply(g, 1, h)
 
         sum_e = const.tile([P, IMAGES * BANKS], F32)
         sum_ey = const.tile([P, IMAGES * BANKS], F32)

@@ -34,6 +34,7 @@ SETS = 4
 SET_GROUPS = GROUPS // SETS
 SCALE_SHIFT = 4
 
+LAG = 2
 RUN = 4
 
 FLOPS = 2 * IMAGES * POSITIONS * (2 * STREAM_CHANNELS) * (WEIGHTS * OUT_CHANNELS)
@@ -57,7 +58,7 @@ def tile_fr_pa_k_kernel(
     ) as weights, tc.tile_pool(name="raw", bufs=6) as raw_pool, tc.tile_pool(
         name="grouped", bufs=4
     ) as grouped_pool, tc.tile_pool(name="quantised", bufs=16) as quantised, tc.tile_pool(
-        name="pooling", bufs=BANKS
+        name="pooling", bufs=IMAGES * BANKS
     ) as pooling, tc.psum_pool(name="acc", bufs=1) as acc_pool, tc.psum_pool(
         name="flip", bufs=1
     ) as flip_pool, tc.manual_schedule():
@@ -91,8 +92,11 @@ def tile_fr_pa_k_kernel(
                         ].bitcast(F32),
                     )
 
-        pooled = const.tile([P, P], F32)
-        nc.vector.memset(pooled[:], 0.0)
+        sum_e = const.tile([P, IMAGES * BANKS], F32)
+        one_over_sum_e = const.tile([P, P], F32)
+        sum_ey = const.tile([P, P], F32)
+        nc.vector.memset(one_over_sum_e[:], 0.0)
+        nc.vector.memset(sum_ey[:], 0.0)
 
         bias_rows_f32 = const.tile([P, P], F32)
         nc.vector.tensor_copy(out=bias_rows_f32[:], in_=bias_rows[:])
@@ -126,9 +130,9 @@ def tile_fr_pa_k_kernel(
                 in_=word_views[c][:, PAIR * pair : PAIR * (pair + 1), :].bitcast(I32),
             )
 
-        def regroup(g, copy):
+        def regroup(g, copies):
             grouped = grouped_pool.tile([P, IMAGES, POSITIONS, PACK], BF16, name="grouped", align_bytes=64)
-            for n in range(IMAGES):
+            for n, copy in enumerate(copies):
                 copy(
                     out=grouped[:, n].rearrange("p (c i) t -> p c t i", i=RUN),
                     in_=raw_tiles[g][:, n].rearrange("p (t c i) -> p c t i", t=PACK, i=RUN),
@@ -171,10 +175,17 @@ def tile_fr_pa_k_kernel(
                     load_x(PAIR * (position // WEIGHTS + 1) + i)
             load_weights(pair, c)
             if c == 0:
-                regroup(PAIR * pair, nc.scalar.copy)
-                regroup(PAIR * pair + 1, nc.vector.tensor_copy)
-                quantise(PAIR * pair)
-                quantise(PAIR * pair + 1)
+                by_scalar, by_vector = nc.scalar.copy, nc.vector.tensor_copy
+                even, odd = PAIR * pair, PAIR * pair + 1
+                if pair < PAIRS - 1:
+                    regroup(even, (by_scalar, by_scalar))
+                    regroup(odd, (by_vector, by_vector))
+                    quantise(even)
+                    quantise(odd)
+                else:
+                    for g in (even, odd):
+                        regroup(g, (by_scalar, by_vector))
+                        quantise(g)
             if pair < PAIRS - TAIL or c == 0:
                 for h in range(HALVES):
                     for i in range(PAIR):
@@ -183,65 +194,69 @@ def tile_fr_pa_k_kernel(
             for g in range(PAIR * (PAIRS - TAIL), GROUPS):
                 multiply(g, 1, h)
 
-        sum_e = const.tile([P, IMAGES * BANKS], F32)
-        sum_ey = const.tile([P, IMAGES * BANKS], F32)
+        units = [(bank, n) for bank in range(BANKS) for n in range(IMAGES)]
         a_tiles = {}
         neg_max_tiles = {}
 
-        def first_exponential(bank):
-            a = pooling.tile([P, IMAGES, POSITIONS], F32, name="a")
+        def first_exponential(bank, n):
+            a = pooling.tile([P, POSITIONS], F32, name="a")
             nc.scalar.activation(
-                out=a[:].rearrange("p n w -> p (n w)"),
-                in_=acc[bank][:],
+                out=a[:],
+                in_=acc[bank][:, POSITIONS * n : POSITIONS * (n + 1)],
                 func=EXP,
                 bias=bias[:, bank : bank + 1],
             )
-            neg_max = pooling.tile([P, IMAGES], F32, name="neg_max")
+            neg_max = pooling.tile([P, 1], F32, name="neg_max")
             nc.vector.tensor_reduce(
                 out=neg_max[:], in_=a[:], axis=mybir.AxisListType.X, op=ALU.max, negate=True
             )
-            a_tiles[bank] = a
-            neg_max_tiles[bank] = neg_max
+            a_tiles[bank, n] = a
+            neg_max_tiles[bank, n] = neg_max
 
-        def second_exponential(bank):
-            e = pooling.tile([P, IMAGES, POSITIONS], F32, name="e")
-            ey = pooling.tile([P, IMAGES, POSITIONS], F32, name="ey")
+        def second_exponential(bank, n):
+            e = pooling.tile([P, POSITIONS], F32, name="e")
+            ey = pooling.tile([P, POSITIONS], F32, name="ey")
             c, h = divmod(bank, HALVES)
-            for n in range(IMAGES):
-                column = (c * IMAGES + n) * HALVES + h
-                nc.scalar.activation(
-                    out=e[:, n],
-                    in_=a_tiles[bank][:, n],
-                    func=EXP,
-                    bias=neg_max_tiles[bank][:, n : n + 1],
-                    accum_out=sum_e[:, column : column + 1],
-                )
-            for n in range(IMAGES):
-                column = (c * IMAGES + n) * HALVES + h
-                nc.vector.scalar_tensor_tensor(
-                    out=ey[:, n],
-                    in0=acc[bank][:, POSITIONS * n : POSITIONS * (n + 1)],
-                    scalar=bias[:, bank : bank + 1],
-                    in1=e[:, n],
-                    op0=ALU.add,
-                    op1=ALU.mult,
-                    accum_out=sum_ey[:, column : column + 1],
-                )
+            column = (c * IMAGES + n) * HALVES + h
+            nc.scalar.activation(
+                out=e[:],
+                in_=a_tiles[bank, n][:],
+                func=EXP,
+                bias=neg_max_tiles[bank, n][:],
+                accum_out=sum_e[:, column : column + 1],
+            )
+            nc.vector.reciprocal(
+                out=one_over_sum_e[:, column : column + 1], in_=sum_e[:, column : column + 1]
+            )
+            nc.vector.scalar_tensor_tensor(
+                out=ey[:],
+                in0=acc[bank][:, POSITIONS * n : POSITIONS * (n + 1)],
+                scalar=bias[:, bank : bank + 1],
+                in1=e[:],
+                op0=ALU.add,
+                op1=ALU.mult,
+                accum_out=sum_ey[:, column : column + 1],
+            )
 
-        for bank in range(BANKS + 1):
-            if bank < BANKS:
-                first_exponential(bank)
-            if bank >= 1:
-                second_exponential(bank - 1)
+        for i in range(len(units) + LAG):
+            if i < len(units):
+                first_exponential(*units[i])
+            if i >= LAG:
+                second_exponential(*units[i - LAG])
 
-        one_over_sum_e = const.tile([P, IMAGES * BANKS], F32)
-        nc.vector.reciprocal(out=one_over_sum_e[:], in_=sum_e[:])
-        nc.vector.tensor_mul(out=pooled[:, 0 : IMAGES * BANKS], in0=sum_ey[:], in1=one_over_sum_e[:])
-
-        pooled_flipped = flip_pool.tile([P, P], F32)
-        nc.tensor.transpose(pooled_flipped[:], pooled[:], identity[:])
+        results = IMAGES * BANKS
+        inverse_flipped = flip_pool.tile([P, P], F32)
+        nc.tensor.transpose(inverse_flipped[:], one_over_sum_e[:], identity[:])
+        sum_ey_flipped = flip_pool.tile([P, P], F32)
+        nc.tensor.transpose(sum_ey_flipped[:], sum_ey[:], identity[:])
+        inverse_rows = const.tile([P, P], F32)
+        nc.scalar.copy(out=inverse_rows[0:results, :], in_=inverse_flipped[0:results, :])
         out_rows = const.tile([P, P], F32)
-        nc.vector.tensor_copy(out=out_rows[:], in_=pooled_flipped[:])
+        nc.vector.tensor_mul(
+            out=out_rows[0:results, :],
+            in0=sum_ey_flipped[0:results, :],
+            in1=inverse_rows[0:results, :],
+        )
         rows = IMAGES * HALVES
-        for c in range(WEIGHTS):
-            nc.sync.dma_start(out=out_views[c], in_=out_rows[rows * c : rows * (c + 1), :])
+        for c, queue in enumerate((nc.scalar, nc.sync)):
+            queue.dma_start(out=out_views[c], in_=out_rows[rows * c : rows * (c + 1), :])

@@ -117,7 +117,10 @@ def tile_fr_pa_k_kernel(
 
         def load_x(g):
             raw = raw_pool.tile([P, IMAGES, PACK * POSITIONS], BF16, name="raw")
-            nc.sync.dma_start(out=raw[:], in_=x_views[g // STREAM_GROUPS][g % STREAM_GROUPS])
+            for n in range(IMAGES):
+                nc.sync.dma_start(
+                    out=raw[:, n], in_=x_views[g // STREAM_GROUPS][g % STREAM_GROUPS][:, n]
+                )
             raw_tiles[g] = raw
 
         def load_weights(pair, c):

@@ -82,15 +82,20 @@ def tile_fr_pa_k_kernel(
                 )
                 nc.vector.memset(plane[:].rearrange("p g n -> p (g n)").bitcast(I32), 0)
                 w_planes[c, s] = plane
-        for s in range(SETS):
-            for c in range(WEIGHTS):
-                for row in range(QUADRANT_ROWS):
-                    nc.gpsimd.dma_start(
-                        out=w_planes[c, s][SCALE_SHIFT * s + row : P : 32].bitcast(F32),
-                        in_=scale_views[c][
-                            row:SCALE_ROWS:QUADRANT_ROWS, SET_GROUPS * s : SET_GROUPS * (s + 1)
-                        ].bitcast(F32),
-                    )
+        def load_scales(queue, dtype, s, c, row):
+            queue.dma_start(
+                out=w_planes[c, s][SCALE_SHIFT * s + row : P : 32].bitcast(dtype),
+                in_=scale_views[c][
+                    row:SCALE_ROWS:QUADRANT_ROWS, SET_GROUPS * s : SET_GROUPS * (s + 1)
+                ].bitcast(dtype),
+            )
+
+        scale_loads = [
+            (s, c, row) for s in range(SETS) for c in range(WEIGHTS) for row in range(QUADRANT_ROWS)
+        ]
+        for s, c, row in scale_loads[: len(scale_loads) // 2]:
+            load_scales(nc.gpsimd, F32, s, c, row)
+        woven = scale_loads[len(scale_loads) // 2 :]
 
         sum_e = const.tile([P, IMAGES * BANKS], F32)
         one_over_sum_e = const.tile([P, P], F32)
@@ -177,6 +182,8 @@ def tile_fr_pa_k_kernel(
                 for i in range(PAIR):
                     load_x(PAIR * (position // WEIGHTS + 1) + i)
             load_weights(pair, c)
+            if WEIGHTS <= position < WEIGHTS + len(woven):
+                load_scales(nc.sync, I32, *woven[position - WEIGHTS])
             if c == 0:
                 by_scalar, by_vector = nc.scalar.copy, nc.vector.tensor_copy
                 even, odd = PAIR * pair, PAIR * pair + 1

@@ -93,9 +93,9 @@ def tile_fr_pa_k_kernel(
         scale_loads = [
             (s, c, row) for s in range(SETS) for c in range(WEIGHTS) for row in range(QUADRANT_ROWS)
         ]
-        for s, c, row in scale_loads[: len(scale_loads) // 2]:
+        for s, c, row in scale_loads[: WEIGHTS * QUADRANT_ROWS]:
             load_scales(nc.gpsimd, F32, s, c, row)
-        woven = scale_loads[len(scale_loads) // 2 :]
+        woven = scale_loads[WEIGHTS * QUADRANT_ROWS :]
 
         sum_e = const.tile([P, IMAGES * BANKS], F32)
         one_over_sum_e = const.tile([P, P], F32)
@@ -182,8 +182,8 @@ def tile_fr_pa_k_kernel(
                 for i in range(PAIR):
                     load_x(PAIR * (position // WEIGHTS + 1) + i)
             load_weights(pair, c)
-            if WEIGHTS <= position < WEIGHTS + len(woven):
-                load_scales(nc.sync, I32, *woven[position - WEIGHTS])
+            if position < len(woven):
+                load_scales(nc.sync, I32, *woven[position])
             if c == 0:
                 by_scalar, by_vector = nc.scalar.copy, nc.vector.tensor_copy
                 even, odd = PAIR * pair, PAIR * pair + 1

@@ -78,7 +78,7 @@ def tile_fr_pa_k_kernel(
         for s in range(SETS):
             for c in range(WEIGHTS):
                 plane = const.tile(
-                    [P, SET_GROUPS, OUT_CHANNELS], U8, name="w_plane%d_%d" % (c, s), align_bytes=64
+                    [P, SET_GROUPS, OUT_CHANNELS], U8, name="w_plane%d_%d" % (c, s), align_bytes=256
                 )
                 nc.vector.memset(plane[:].rearrange("p g n -> p (g n)").bitcast(I32), 0)
                 w_planes[c, s] = plane
@@ -121,7 +121,9 @@ def tile_fr_pa_k_kernel(
         w_words = {}
 
         def load_x(g):
-            raw = raw_pool.tile([P, IMAGES, PACK * POSITIONS], BF16, name="raw")
+            raw = raw_pool.tile(
+                [P, IMAGES, PACK * POSITIONS], BF16, name="raw", align_bytes=256
+            )
             for n in range(IMAGES):
                 nc.sync.dma_start(
                     out=raw[:, n], in_=x_views[g // STREAM_GROUPS][g % STREAM_GROUPS][:, n]
@@ -131,7 +133,7 @@ def tile_fr_pa_k_kernel(
         def load_weights(pair, c):
             if pair not in w_words:
                 w_words[pair] = weights.tile(
-                    [P, WEIGHTS, PAIR, OUT_CHANNELS], U32, name="words", align_bytes=64
+                    [P, WEIGHTS, PAIR, OUT_CHANNELS], U32, name="words", align_bytes=256
                 )
             nc.sync.dma_start(
                 out=w_words[pair][:, c].bitcast(I32),

@@ -180,9 +180,13 @@ def tile_fr_pa_k_kernel(
         for g in range(PAIR):
             load_x(g)
         for position, (pair, c) in enumerate(order):
-            if position % WEIGHTS == 0 and position < WEIGHTS * (PAIRS - 1):
+            if c == 0 and pair < PAIRS - TAIL:
                 for i in range(PAIR):
-                    load_x(PAIR * (position // WEIGHTS + 1) + i)
+                    load_x(PAIR * (pair + 1) + i)
+            if (pair, c) == (PAIRS - TAIL - 1, WEIGHTS - 1):
+                load_x(GROUPS - 2)
+            if (pair, c) == (PAIRS - TAIL, 0):
+                load_x(GROUPS - 1)
             load_weights(pair, c)
             if position < len(woven):
                 load_scales(nc.sync, I32, *woven[position])
@@ -211,18 +215,25 @@ def tile_fr_pa_k_kernel(
         neg_max_tiles = {}
 
         def first_exponential(bank, n):
-            a = pooling.tile([P, POSITIONS], F32, name="a")
-            nc.scalar.activation(
-                out=a[:],
-                in_=acc[bank][:, POSITIONS * n : POSITIONS * (n + 1)],
-                func=EXP,
-                bias=bias[:, bank : bank + 1],
-            )
+            if bank == 0 or n == 0:
+                images = 1 if bank == 0 else IMAGES
+                a = pooling.tile([P, IMAGES, POSITIONS], F32, name="a")
+                nc.scalar.activation(
+                    out=a[:, n : n + images].rearrange("p n w -> p (n w)"),
+                    in_=acc[bank][:, POSITIONS * n : POSITIONS * (n + images)],
+                    func=EXP,
+                    bias=bias[:, bank : bank + 1],
+                )
+                for m in range(n, n + images):
+                    a_tiles[bank, m] = a
             neg_max = pooling.tile([P, 1], F32, name="neg_max")
             nc.vector.tensor_reduce(
-                out=neg_max[:], in_=a[:], axis=mybir.AxisListType.X, op=ALU.max, negate=True
+                out=neg_max[:],
+                in_=a_tiles[bank, n][:, n],
+                axis=mybir.AxisListType.X,
+                op=ALU.max,
+                negate=True,
             )
-            a_tiles[bank, n] = a
             neg_max_tiles[bank, n] = neg_max
 
         def second_exponential(bank, n):
@@ -232,14 +243,16 @@ def tile_fr_pa_k_kernel(
             column = (c * IMAGES + n) * HALVES + h
             nc.scalar.activation(
                 out=e[:],
-                in_=a_tiles[bank, n][:],
+                in_=a_tiles[bank, n][:, n],
                 func=EXP,
                 bias=neg_max_tiles[bank, n][:],
                 accum_out=sum_e[:, column : column + 1],
             )
-            nc.vector.reciprocal(
-                out=one_over_sum_e[:, column : column + 1], in_=sum_e[:, column : column + 1]
-            )
+            if h == HALVES - 1 and n == IMAGES - 1:
+                first = c * IMAGES * HALVES
+                nc.vector.reciprocal(
+                    out=one_over_sum_e[:, first : column + 1], in_=sum_e[:, first : column + 1]
+                )
             nc.vector.scalar_tensor_tensor(
                 out=ey[:],
                 in0=acc[bank][:, POSITIONS * n : POSITIONS * (n + 1)],

import concourse.mybir as mybir
from concourse.masks import make_identity

F32 = mybir.dt.float32
BF16 = mybir.dt.bfloat16
I32 = mybir.dt.int32
U32 = mybir.dt.uint32
U8 = mybir.dt.uint8
FP8X4 = mybir.dt.float8_e4m3fn_x4
EXP = mybir.ActivationFunctionType.Exp
ALU = mybir.AluOpType

P = 128
PACK = 4
K_GROUP = P * PACK

IMAGES = 2
STREAM_CHANNELS = 8192
POSITIONS = 256
COLUMNS = IMAGES * POSITIONS
OUT_CHANNELS = 256
WEIGHTS = 2
HALVES = OUT_CHANNELS // P
BANKS = WEIGHTS * HALVES

STREAM_GROUPS = STREAM_CHANNELS // K_GROUP
GROUPS = 2 * STREAM_GROUPS
PAIR = 2
PAIRS = GROUPS // PAIR
TAIL = 2
SCALE_ROWS = 16
QUADRANT_ROWS = 4
SETS = 4
SET_GROUPS = GROUPS // SETS
SCALE_SHIFT = 4

LAG = 2
RUN = 4

FLOPS = 2 * IMAGES * POSITIONS * (2 * STREAM_CHANNELS) * (WEIGHTS * OUT_CHANNELS)


def tile_fr_pa_k_kernel(
    tc, x1, x2, c1_w_words, c1_w_scales, c1_b, c2_w_words, c2_w_scales, c2_b, out_0, out_1
):
    nc = tc.nc

    x_views = [
        x.rearrange("n (g p t) h w -> g p n (t h w)", p=P, t=PACK) for x in (x1, x2)
    ]
    word_views = [w.rearrange("g p n t -> p g (n t)") for w in (c1_w_words, c2_w_words)]
    scale_views = [s.rearrange("g q n -> q g n") for s in (c1_w_scales, c2_w_scales)]
    bias_views = [b.rearrange("(h p) -> h p", p=P) for b in (c1_b, c2_b)]
    out_views = [o.rearrange("n (h p) -> (n h) p", p=P) for o in (out_0, out_1)]

    with tc.tile_pool(name="const", bufs=1) as const, tc.tile_pool(
        name="weights", bufs=PAIRS
    ) as weights, tc.tile_pool(name="raw", bufs=6) as raw_pool, tc.tile_pool(
        name="grouped", bufs=4
    ) as grouped_pool, tc.tile_pool(name="quantised", bufs=16) as quantised, tc.tile_pool(
        name="pooling", bufs=IMAGES * BANKS
    ) as pooling, tc.psum_pool(name="acc", bufs=1) as acc_pool, tc.psum_pool(
        name="flip", bufs=1
    ) as flip_pool, tc.manual_schedule():
        bias_rows = const.tile([P, P], BF16)
        nc.vector.memset(bias_rows[:], 0.0)
        for c in range(WEIGHTS):
            nc.scalar.dma_start(out=bias_rows[HALVES * c : HALVES * (c + 1), :], in_=bias_views[c])

        table_warm = const.tile([P, 1], F32)
        nc.vector.memset(table_warm[:], 0.0)
        nc.scalar.activation(out=table_warm[:], in_=table_warm[:], func=EXP)

        identity = const.tile([P, P], F32)
        make_identity(nc, identity[:])

        w_planes = {}
        for s in range(SETS):
            for c in range(WEIGHTS):
                plane = const.tile(
                    [P, SET_GROUPS, OUT_CHANNELS], U8, name="w_plane%d_%d" % (c, s), align_bytes=256
                )
                nc.vector.memset(plane[:].rearrange("p g n -> p (g n)").bitcast(I32), 0)
                w_planes[c, s] = plane
        def load_scales(queue, dtype, s, c, row):
            queue.dma_start(
                out=w_planes[c, s][SCALE_SHIFT * s + row : P : 32].bitcast(dtype),
                in_=scale_views[c][
                    row:SCALE_ROWS:QUADRANT_ROWS, SET_GROUPS * s : SET_GROUPS * (s + 1)
                ].bitcast(dtype),
            )

        scale_loads = [
            (s, c, row) for s in range(SETS) for c in range(WEIGHTS) for row in range(QUADRANT_ROWS)
        ]
        for s, c, row in scale_loads[: WEIGHTS * QUADRANT_ROWS]:
            load_scales(nc.gpsimd, F32, s, c, row)
        woven = scale_loads[WEIGHTS * QUADRANT_ROWS :]

        sum_e = const.tile([P, IMAGES * BANKS], F32)
        one_over_sum_e = const.tile([P, P], F32)
        sum_ey = const.tile([P, P], F32)
        nc.vector.memset(one_over_sum_e[:], 0.0)
        nc.vector.memset(sum_ey[:], 0.0)

        bias_rows_f32 = const.tile([P, P], F32)
        nc.vector.tensor_copy(out=bias_rows_f32[:], in_=bias_rows[:])
        bias_flipped = flip_pool.tile([P, P], F32)
        nc.tensor.transpose(bias_flipped[:], bias_rows_f32[:], identity[:])
        bias = const.tile([P, BANKS], F32)
        nc.vector.tensor_copy(out=bias[:], in_=bias_flipped[:, 0:BANKS])

        acc = [
            acc_pool.tile([P, COLUMNS], F32, name="acc%d" % bank) for bank in range(BANKS)
        ]

        raw_tiles = {}
        grouped_tiles = {}
        x_words = {}
        x_planes = {}
        w_words = {}

        def load_x(g):
            raw = raw_pool.tile(
                [P, IMAGES, PACK * POSITIONS], BF16, name="raw", align_bytes=256
            )
            for n in range(IMAGES):
                nc.sync.dma_start(
                    out=raw[:, n], in_=x_views[g // STREAM_GROUPS][g % STREAM_GROUPS][:, n]
                )
            raw_tiles[g] = raw

        def load_weights(pair, c):
            if pair not in w_words:
                w_words[pair] = weights.tile(
                    [P, WEIGHTS, PAIR, OUT_CHANNELS], U32, name="words", align_bytes=256
                )
            nc.sync.dma_start(
                out=w_words[pair][:, c].bitcast(I32),
                in_=word_views[c][:, PAIR * pair : PAIR * (pair + 1), :].bitcast(I32),
            )

        def regroup(g, copies):
            grouped = grouped_pool.tile([P, IMAGES, POSITIONS, PACK], BF16, name="grouped", align_bytes=64)
            for n, copy in enumerate(copies):
                copy(
                    out=grouped[:, n].rearrange("p (c i) t -> p c t i", i=RUN),
                    in_=raw_tiles[g][:, n].rearrange("p (t c i) -> p c t i", t=PACK, i=RUN),
                )
            grouped_tiles[g] = grouped

        def quantise(g):
            words = quantised.tile([P, COLUMNS], U32, name="x_words", align_bytes=64)
            plane = quantised.tile([P, COLUMNS], U8, name="x_plane", align_bytes=64)
            nc.vector.quantize_mx(
                out=words[:].bitcast(FP8X4),
                scales=plane[:],
                in_=grouped_tiles[g][:].rearrange("p n w t -> p (n w t)"),
            )
            x_words[g] = words
            x_planes[g] = plane

        def multiply(g, c, h):
            pair, i = divmod(g, PAIR)
            nc.tensor.matmul_mx(
                out=acc[HALVES * c + h][:],
                lhsT=w_words[pair][:, c, i, P * h : P * (h + 1)].bitcast(FP8X4),
                lhsT_scale=w_planes[c, g // SET_GROUPS][
                    SCALE_SHIFT * (g // SET_GROUPS) : P, g % SET_GROUPS, P * h : P * (h + 1)
                ],
                rhs=x_words[g][:].bitcast(FP8X4),
                rhs_scale=x_planes[g][:],
                start=(g == 0),
                stop=(g == GROUPS - 1),
            )

        order = [(pair, c) for pair in range(PAIRS - TAIL) for c in range(WEIGHTS)] + [
            (pair, c) for c in range(WEIGHTS) for pair in range(PAIRS - TAIL, PAIRS)
        ]
        for g in range(PAIR):
            load_x(g)
        for position, (pair, c) in enumerate(order):
            if c == 0 and pair < PAIRS - TAIL:
                for i in range(PAIR):
                    load_x(PAIR * (pair + 1) + i)
            if (pair, c) == (PAIRS - TAIL - 1, WEIGHTS - 1):
                load_x(GROUPS - 2)
            if (pair, c) == (PAIRS - TAIL, 0):
                load_x(GROUPS - 1)
            load_weights(pair, c)
            if position < len(woven):
                load_scales(nc.sync, I32, *woven[position])
            if c == 0:
                by_scalar, by_vector = nc.scalar.copy, nc.vector.tensor_copy
                even, odd = PAIR * pair, PAIR * pair + 1
                if pair < PAIRS - 1:
                    regroup(even, (by_scalar, by_scalar))
                    regroup(odd, (by_vector, by_vector))
                    quantise(even)
                    quantise(odd)
                else:
                    for g in (even, odd):
                        regroup(g, (by_scalar, by_vector))
                        quantise(g)
            if pair < PAIRS - TAIL or c == 0:
                for h in range(HALVES):
                    for i in range(PAIR):
                        multiply(PAIR * pair + i, c, h)
        for h in range(HALVES):
            for g in range(PAIR * (PAIRS - TAIL), GROUPS):
                multiply(g, 1, h)

        units = [(bank, n) for bank in range(BANKS) for n in range(IMAGES)]
        a_tiles = {}
        neg_max_tiles = {}

        def first_exponential(bank, n):
            if bank == 0 or n == 0:
                images = 1 if bank == 0 else IMAGES
                a = pooling.tile([P, IMAGES, POSITIONS], F32, name="a")
                nc.scalar.activation(
                    out=a[:, n : n + images].rearrange("p n w -> p (n w)"),
                    in_=acc[bank][:, POSITIONS * n : POSITIONS * (n + images)],
                    func=EXP,
                    bias=bias[:, bank : bank + 1],
                )
                for m in range(n, n + images):
                    a_tiles[bank, m] = a
            neg_max = pooling.tile([P, 1], F32, name="neg_max")
            nc.vector.tensor_reduce(
                out=neg_max[:],
                in_=a_tiles[bank, n][:, n],
                axis=mybir.AxisListType.X,
                op=ALU.max,
                negate=True,
            )
            neg_max_tiles[bank, n] = neg_max

        def second_exponential(bank, n):
            e = pooling.tile([P, POSITIONS], F32, name="e")
            ey = pooling.tile([P, POSITIONS], F32, name="ey")
            c, h = divmod(bank, HALVES)
            column = (c * IMAGES + n) * HALVES + h
            nc.scalar.activation(
                out=e[:],
                in_=a_tiles[bank, n][:, n],
                func=EXP,
                bias=neg_max_tiles[bank, n][:],
                accum_out=sum_e[:, column : column + 1],
            )
            if h == HALVES - 1 and n == IMAGES - 1:
                first = c * IMAGES * HALVES
                nc.vector.reciprocal(
                    out=one_over_sum_e[:, first : column + 1], in_=sum_e[:, first : column + 1]
                )
            nc.vector.scalar_tensor_tensor(
                out=ey[:],
                in0=acc[bank][:, POSITIONS * n : POSITIONS * (n + 1)],
                scalar=bias[:, bank : bank + 1],
                in1=e[:],
                op0=ALU.add,
                op1=ALU.mult,
                accum_out=sum_ey[:, column : column + 1],
            )

        for i in range(len(units) + LAG):
            if i < len(units):
                first_exponential(*units[i])
            if i >= LAG:
                second_exponential(*units[i - LAG])

        results = IMAGES * BANKS
        inverse_flipped = flip_pool.tile([P, P], F32)
        nc.tensor.transpose(inverse_flipped[:], one_over_sum_e[:], identity[:])
        sum_ey_flipped = flip_pool.tile([P, P], F32)
        nc.tensor.transpose(sum_ey_flipped[:], sum_ey[:], identity[:])
        inverse_rows = const.tile([P, P], F32)
        nc.scalar.copy(out=inverse_rows[0:results, :], in_=inverse_flipped[0:results, :])
        out_rows = const.tile([P, P], F32)
        nc.vector.tensor_mul(
            out=out_rows[0:results, :],
            in0=sum_ey_flipped[0:results, :],
            in1=inverse_rows[0:results, :],
        )
        rows = IMAGES * HALVES
        for c, queue in enumerate((nc.scalar, nc.sync)):
            queue.dma_start(out=out_views[c], in_=out_rows[rows * c : rows * (c + 1), :])
